import numpy as np
import ml_dtypes


def mxq(x, axis, fmt="e4m3"):
    dtype, down = {"e4m3": (ml_dtypes.float8_e4m3fn, 7), "e5m2": (ml_dtypes.float8_e5m2, 14)}[fmt]
    v = np.moveaxis(np.asarray(x, np.float32).astype(ml_dtypes.bfloat16).astype(np.float64), axis, -1)
    blocks = v.reshape(v.shape[:-1] + (-1, 32))
    amax = np.abs(blocks).max(-1, keepdims=True)
    byte = np.maximum(np.where(amax > 0, np.frexp(amax)[1] - 1 + 127, 0) - down, 1)
    scale = np.exp2(byte - 127.0)
    codes = (blocks / scale).astype(np.float32).astype(dtype).astype(np.float64)
    return np.moveaxis((codes * scale).reshape(v.shape), -1, axis)


WIDE = False


def mx_kscale(k):
    if not WIDE:
        return np.ones(k)
    levels = np.array([20, -20, 10, -10, 0])
    a = np.random.permutation(np.resize(levels, k // 512 * 4)).reshape(k // 512, 4)
    idx = np.arange(k)
    return np.exp2(a[idx // 512, idx % 128 // 32])


BF16 = ml_dtypes.bfloat16


def bf(x):
    return np.asarray(x, np.float32).astype(BF16)


def f64(x):
    return np.asarray(x).astype(np.float64)


B, N, IN, OUT = 8, 1024, 512, 512


def setup_inputs():
    u = mx_kscale(OUT)
    x = np.random.standard_normal((B, N, IN))
    weight = np.random.standard_normal((IN, OUT)) * 0.7 / np.sqrt(IN) / u
    bias = np.random.standard_normal((1, OUT)) * 0.5
    sigma_weight = (1.0 + 0.3 * np.random.standard_normal((IN, OUT))) * 0.7 / np.sqrt(IN) / u
    sigma_bias = (1.0 + 0.3 * np.random.standard_normal((1, OUT))) * 0.5
    weight_epsilon = np.random.standard_normal((B, IN, OUT))
    bias_epsilon = np.random.standard_normal((B, 1, OUT))
    g = np.random.standard_normal((B, N, OUT)) * np.exp2(np.random.randint(-12, 1, (B, N, 1))) * 4.0 * u
    return {
        "x": bf(x),
        "weight": bf(weight),
        "bias": bf(bias),
        "sigma_weight": bf(sigma_weight),
        "sigma_bias": bf(sigma_bias),
        "weight_epsilon": bf(weight_epsilon),
        "bias_epsilon": bf(bias_epsilon),
        "grad_out": bf(g),
    }


def reference(x, weight, bias, sigma_weight, sigma_bias, weight_epsilon, bias_epsilon, grad_out):
    noisy_w = f64(weight) + f64(weight_epsilon) * f64(sigma_weight)
    return mxq(f64(grad_out), 2, "e5m2") @ mxq(noisy_w, 2, "e4m3").transpose(0, 2, 1)

@@ -1,0 +1,186 @@
+from contextlib import ExitStack
+
+import concourse.mybir as mybir
+from concourse.masks import make_identity
+
+B, N, IN, OUT = 8, 1024, 512, 512
+FLOPS = 2 * B * N * IN * OUT
+BYTES = B * N * OUT * 2 + B * IN * OUT * 2 + 2 * IN * OUT * 2 + B * N * IN * 4
+
+F32 = mybir.dt.float32
+BF16 = mybir.dt.bfloat16
+U32 = mybir.dt.uint32
+U8 = mybir.dt.uint8
+E4 = mybir.dt.float8_e4m3fn_x4
+E5 = mybir.dt.float8_e5m2_x4
+P = 128
+TT = N // P
+WT = IN // P
+MULT = mybir.AluOpType.mult
+ADD = mybir.AluOpType.add
+
+
+def tile_noisylinear_t_kernel(
+    tc, x, weight, bias, sigma_weight, sigma_bias, weight_epsilon, bias_epsilon, grad_out, out
+):
+    nc = tc.nc
+    with ExitStack() as ctx:
+        const = ctx.enter_context(tc.tile_pool(name="const", bufs=1))
+        gload = ctx.enter_context(tc.tile_pool(name="gload", bufs=B))
+        eload = ctx.enter_context(tc.tile_pool(name="eload", bufs=B + 2))
+        work = ctx.enter_context(tc.tile_pool(name="work", bufs=2))
+        stage = ctx.enter_context(tc.tile_pool(name="stage", bufs=6))
+        ps_g = ctx.enter_context(tc.psum_pool(name="ps_g", bufs=2))
+        ps_e = ctx.enter_context(tc.psum_pool(name="ps_e", bufs=2))
+        ps_o = ctx.enter_context(tc.psum_pool(name="ps_o", bufs=4))
+
+        ident = const.tile([P, P], F32, name="ident")
+        make_identity(nc, ident[:])
+
+        g_sb = []
+        e_sb = []
+        for b in range(B):
+            g_t = gload.tile([P, TT, OUT], BF16, name="g_t", tag="g")
+            g_sb.append(g_t)
+            e_t = eload.tile([P, WT, OUT], BF16, name="e_t", tag="e")
+            e_sb.append(e_t)
+        s_raw = eload.tile([P, WT, OUT], BF16, name="s_raw", tag="e")
+        w_raw = eload.tile([P, WT, OUT], BF16, name="w_raw", tag="e")
+
+        def load_g(b, lo, hi):
+            nc.sync.dma_start(
+                out=g_sb[b][:, lo:hi, :],
+                in_=grad_out[b].rearrange("(p t) k -> p t k", t=TT)[:, lo:hi, :],
+            )
+
+        def load_w(dst, src):
+            nc.sync.dma_start(out=dst[:], in_=src.rearrange("(p t) k -> p t k", t=WT))
+
+        load_g(0, 0, 4)
+        load_w(s_raw, sigma_weight)
+        load_w(e_sb[0], weight_epsilon[0])
+        load_w(w_raw, weight)
+        load_g(0, 4, 8)
+        for b in range(1, B):
+            load_w(e_sb[b], weight_epsilon[b])
+            load_g(b, 0, 8)
+
+        def transpose_w(src):
+            src32 = src[:].bitcast(F32)
+            banks = []
+            for h in range(2):
+                xe = ps_e.tile([P, 512], F32, name="xe", tag="xe")
+                for s in range(4):
+                    t, u = (4 * h + s) // 2, s % 2
+                    nc.tensor.transpose(
+                        xe[:, s * P : (s + 1) * P], src32[:, t, u * P : (u + 1) * P], ident[:]
+                    )
+                banks.append(xe)
+            return banks
+
+        def prep_const(src, name):
+            dst = const.tile([P, P, 16], BF16, name=name, align_bytes=64)
+            banks = transpose_w(src)
+            for h in range(2):
+                nc.vector.tensor_copy(
+                    out=dst[:].bitcast(F32)[:, :, 4 * h : 4 * h + 4],
+                    in_=banks[h][:].rearrange("p (s c) -> p c s", s=4),
+                )
+            return dst
+
+        state = {}
+
+        def stage_g(b):
+            g32 = g_sb[b][:].bitcast(F32)
+            gg = work.tile([P, TT, P, 4], BF16, name="gg", tag="gg", align_bytes=64)
+            gg32 = gg[:].bitcast(F32)
+            for j in range(TT // 2):
+                xg = ps_g.tile([P, 512], F32, name="xg", tag="xg")
+                for s in range(4):
+                    t, u = 2 * j + s // 2, s % 2
+                    nc.tensor.transpose(
+                        xg[:, s * P : (s + 1) * P], g32[:, t, u * P : (u + 1) * P], ident[:]
+                    )
+                nc.scalar.copy(
+                    out=gg32[:, 2 * j : 2 * j + 2, :, :],
+                    in_=xg[:].rearrange("p (t u c) -> p t c u", t=2, u=2),
+                )
+            gc = work.tile([P, N], U32, name="gc", tag="gc", align_bytes=64)
+            gs = work.tile([P, N], U8, name="gs", tag="gs", align_bytes=64)
+            state[("g", b)] = (gg, gc, gs)
+
+        def quant_g(b):
+            gg, gc, gs = state[("g", b)]
+            nc.vector.quantize_mx(
+                out=gc[:].bitcast(E5), scales=gs[:], in_=gg[:].rearrange("p t c j -> p (t c j)")
+            )
+
+        def stage_w(b):
+            banks = transpose_w(e_sb[b])
+            pr = work.tile([P, P, 8, 2], F32, name="pr", tag="pr")
+            for h in range(2):
+                nc.vector.tensor_tensor(
+                    out=pr[:, :, 4 * h : 4 * h + 4, :],
+                    in0=banks[h][:].bitcast(BF16).rearrange("p (s c e) -> p c s e", s=4, e=2),
+                    in1=sig_g[:, :, 8 * h : 8 * h + 8].rearrange("p c (s e) -> p c s e", e=2),
+                    op=MULT,
+                )
+            state[("p", b)] = pr
+
+        def add_w(b):
+            pr = state[("p", b)]
+            ng = work.tile([P, 4 * IN], BF16, name="ng", tag="ng", align_bytes=64)
+            nc.vector.tensor_tensor(
+                out=ng[:],
+                in0=pr[:].rearrange("p c s e -> p (c s e)"),
+                in1=w_g[:].rearrange("p c j -> p (c j)"),
+                op=ADD,
+            )
+            state[("n", b)] = ng
+
+        def quant_w(b):
+            ng = state[("n", b)]
+            ncod = work.tile([P, IN], U32, name="ncod", tag="ncod", align_bytes=64)
+            nsc = work.tile([P, IN], U8, name="nsc", tag="nsc", align_bytes=64)
+            nc.vector.quantize_mx(out=ncod[:].bitcast(E4), scales=nsc[:], in_=ng[:])
+            state[("q", b)] = (ncod, nsc)
+
+        def stage_mm(b):
+            gg, gc, gs = state[("g", b)]
+            ncod, nsc = state[("q", b)]
+            out_v = out[b].rearrange("(p t) i -> p t i", t=TT)
+            for h in range(2):
+                o_sb = stage.tile([P, 4, IN], F32, name="o_sb", tag="o")
+                for r in range(4):
+                    t = 4 * h + r
+                    acc = ps_o.tile([P, IN], F32, name="acc", tag="acc")
+                    nc.tensor.matmul_mx(
+                        out=acc[:],
+                        lhsT=gc[:, t * P : (t + 1) * P].bitcast(E5),
+                        lhsT_scale=gs[:, t * P : (t + 1) * P],
+                        rhs=ncod[:].bitcast(E4),
+                        rhs_scale=nsc[:],
+                        start=True,
+                        stop=True,
+                    )
+                    nc.scalar.copy(out=o_sb[:, r, :], in_=acc[:])
+                nc.gpsimd.dma_start(out=out_v[:, 4 * h : 4 * h + 4, :], in_=o_sb[:])
+
+        def stage_a(b):
+            stage_g(b)
+            stage_w(b)
+            quant_g(b)
+            add_w(b)
+            quant_w(b)
+
+        stage_g(0)
+        sig_g = prep_const(s_raw, "sig_g")
+        stage_w(0)
+        w_g = prep_const(w_raw, "w_g")
+        quant_g(0)
+        add_w(0)
+        quant_w(0)
+        for b in range(B):
+            if b + 1 < B:
+                stage_a(b + 1)
+            stage_mm(b)

@@ -18,6 +18,14 @@ TT = N // P
 WT = IN // P
 MULT = mybir.AluOpType.mult
 ADD = mybir.AluOpType.add
+POOL_C = 64
+EARLY = 6
+
+
+def vector_rows(b):
+    if b == B - 1:
+        return (1, 3, 5, 7)
+    return (7,)
 
 
 def tile_noisylinear_t_kernel(
@@ -26,161 +34,236 @@ def tile_noisylinear_t_kernel(
     nc = tc.nc
     with ExitStack() as ctx:
         const = ctx.enter_context(tc.tile_pool(name="const", bufs=1))
-        gload = ctx.enter_context(tc.tile_pool(name="gload", bufs=B))
-        eload = ctx.enter_context(tc.tile_pool(name="eload", bufs=B + 2))
+        gload = ctx.enter_context(tc.tile_pool(name="gload", bufs=7))
+        eload = ctx.enter_context(tc.tile_pool(name="eload", bufs=8))
         work = ctx.enter_context(tc.tile_pool(name="work", bufs=2))
-        stage = ctx.enter_context(tc.tile_pool(name="stage", bufs=6))
-        ps_g = ctx.enter_context(tc.psum_pool(name="ps_g", bufs=2))
+        stage = ctx.enter_context(tc.tile_pool(name="stage", bufs=4))
+        ps_g = ctx.enter_context(tc.psum_pool(name="ps_g", bufs=3))
         ps_e = ctx.enter_context(tc.psum_pool(name="ps_e", bufs=2))
-        ps_o = ctx.enter_context(tc.psum_pool(name="ps_o", bufs=4))
+        ps_o = ctx.enter_context(tc.psum_pool(name="ps_o", bufs=3))
+        ctx.enter_context(tc.manual_schedule())
 
         ident = const.tile([P, P], F32, name="ident")
         make_identity(nc, ident[:])
+        sig_g = const.tile([P, P, 16], BF16, name="sig_g", align_bytes=64)
+        w_g = const.tile([P, P, 16], BF16, name="w_g", align_bytes=64)
 
-        g_sb = []
-        e_sb = []
-        for b in range(B):
-            g_t = gload.tile([P, TT, OUT], BF16, name="g_t", tag="g")
-            g_sb.append(g_t)
-            e_t = eload.tile([P, WT, OUT], BF16, name="e_t", tag="e")
-            e_sb.append(e_t)
-        s_raw = eload.tile([P, WT, OUT], BF16, name="s_raw", tag="e")
-        w_raw = eload.tile([P, WT, OUT], BF16, name="w_raw", tag="e")
+        T = {}
+
+        def ok(b):
+            return 0 <= b < B
 
         def load_g(b, lo, hi):
+            if lo == 0:
+                T["g", b] = gload.tile([P, TT, OUT], BF16, name="g_t", tag="g")
             nc.sync.dma_start(
-                out=g_sb[b][:, lo:hi, :],
+                out=T["g", b][:, lo:hi, :],
                 in_=grad_out[b].rearrange("(p t) k -> p t k", t=TT)[:, lo:hi, :],
             )
 
-        def load_w(dst, src):
-            nc.sync.dma_start(out=dst[:], in_=src.rearrange("(p t) k -> p t k", t=WT))
+        def load_w(key, src):
+            T["e", key] = eload.tile([P, WT, OUT], BF16, name="e_t", tag="e")
+            nc.sync.dma_start(out=T["e", key][:], in_=src.rearrange("(p t) k -> p t k", t=WT))
 
-        load_g(0, 0, 4)
-        load_w(s_raw, sigma_weight)
-        load_w(e_sb[0], weight_epsilon[0])
-        load_w(w_raw, weight)
-        load_g(0, 4, 8)
-        for b in range(1, B):
-            load_w(e_sb[b], weight_epsilon[b])
-            load_g(b, 0, 8)
-
-        def transpose_w(src):
-            src32 = src[:].bitcast(F32)
-            banks = []
-            for h in range(2):
-                xe = ps_e.tile([P, 512], F32, name="xe", tag="xe")
-                for s in range(4):
-                    t, u = (4 * h + s) // 2, s % 2
-                    nc.tensor.transpose(
-                        xe[:, s * P : (s + 1) * P], src32[:, t, u * P : (u + 1) * P], ident[:]
-                    )
-                banks.append(xe)
-            return banks
-
-        def prep_const(src, name):
-            dst = const.tile([P, P, 16], BF16, name=name, align_bytes=64)
-            banks = transpose_w(src)
-            for h in range(2):
-                nc.vector.tensor_copy(
-                    out=dst[:].bitcast(F32)[:, :, 4 * h : 4 * h + 4],
-                    in_=banks[h][:].rearrange("p (s c) -> p c s", s=4),
+        def te(key, h, pool, tag):
+            src32 = T["e", key][:].bitcast(F32)
+            xe = pool.tile([P, 512], F32, name="xe", tag=tag)
+            for s in range(4):
+                t, u = (4 * h + s) // 2, s % 2
+                nc.tensor.transpose(
+                    xe[:, s * P : (s + 1) * P], src32[:, t, u * P : (u + 1) * P], ident[:]
                 )
-            return dst
+            T["xe", key, h] = xe
 
-        state = {}
+        def TE(b, h):
+            if ok(b):
+                te(b, h, ps_e, "xe")
 
-        def stage_g(b):
-            g32 = g_sb[b][:].bitcast(F32)
-            gg = work.tile([P, TT, P, 4], BF16, name="gg", tag="gg", align_bytes=64)
-            gg32 = gg[:].bitcast(F32)
-            for j in range(TT // 2):
-                xg = ps_g.tile([P, 512], F32, name="xg", tag="xg")
-                for s in range(4):
-                    t, u = 2 * j + s // 2, s % 2
-                    nc.tensor.transpose(
-                        xg[:, s * P : (s + 1) * P], g32[:, t, u * P : (u + 1) * P], ident[:]
-                    )
-                nc.scalar.copy(
-                    out=gg32[:, 2 * j : 2 * j + 2, :, :],
-                    in_=xg[:].rearrange("p (t u c) -> p t c u", t=2, u=2),
+        def PC(key, h, dst):
+            nc.scalar.copy(
+                out=dst[:].bitcast(F32)[:, :, 4 * h : 4 * h + 4],
+                in_=T["xe", key, h][:].rearrange("p (s c) -> p c s", s=4),
+            )
+
+        def TG(b, j):
+            if not ok(b):
+                return
+            g32 = T["g", b][:].bitcast(F32)
+            xg = ps_g.tile([P, 512], F32, name="xg", tag="xg")
+            for s in range(4):
+                t, u = 2 * j + s // 2, s % 2
+                nc.tensor.transpose(
+                    xg[:, s * P : (s + 1) * P], g32[:, t, u * P : (u + 1) * P], ident[:]
                 )
+            T["xg", b, j] = xg
+
+        def G(b, j):
+            if not ok(b):
+                return
+            if j == 0:
+                T["gg", b] = work.tile([P, TT, P, 4], BF16, name="gg", tag="gg", align_bytes=64)
+            nc.scalar.copy(
+                out=T["gg", b][:].bitcast(F32)[:, 2 * j : 2 * j + 2, :, :],
+                in_=T["xg", b, j][:].rearrange("p (t u c) -> p t c u", t=2, u=2),
+            )
+
+        def QG(b):
+            if not ok(b):
+                return
             gc = work.tile([P, N], U32, name="gc", tag="gc", align_bytes=64)
             gs = work.tile([P, N], U8, name="gs", tag="gs", align_bytes=64)
-            state[("g", b)] = (gg, gc, gs)
-
-        def quant_g(b):
-            gg, gc, gs = state[("g", b)]
             nc.vector.quantize_mx(
-                out=gc[:].bitcast(E5), scales=gs[:], in_=gg[:].rearrange("p t c j -> p (t c j)")
+                out=gc[:].bitcast(E5),
+                scales=gs[:],
+                in_=T["gg", b][:].rearrange("p t c j -> p (t c j)"),
+            )
+            T["gq", b] = (gc, gs)
+
+        def M(b, h):
+            if not ok(b):
+                return
+            if h == 0:
+                T["pr", b] = work.tile([P, P, 8, 2], F32, name="pr", tag="pr")
+            nc.vector.tensor_tensor(
+                out=T["pr", b][:, :, 4 * h : 4 * h + 4, :],
+                in0=T["xe", b, h][:].bitcast(BF16).rearrange("p (s c e) -> p c s e", s=4, e=2),
+                in1=sig_g[:, :, 8 * h : 8 * h + 8].rearrange("p c (s e) -> p c s e", e=2),
+                op=MULT,
             )
 
-        def stage_w(b):
-            banks = transpose_w(e_sb[b])
-            pr = work.tile([P, P, 8, 2], F32, name="pr", tag="pr")
-            for h in range(2):
-                nc.vector.tensor_tensor(
-                    out=pr[:, :, 4 * h : 4 * h + 4, :],
-                    in0=banks[h][:].bitcast(BF16).rearrange("p (s c e) -> p c s e", s=4, e=2),
-                    in1=sig_g[:, :, 8 * h : 8 * h + 8].rearrange("p c (s e) -> p c s e", e=2),
-                    op=MULT,
-                )
-            state[("p", b)] = pr
-
-        def add_w(b):
-            pr = state[("p", b)]
-            ng = work.tile([P, 4 * IN], BF16, name="ng", tag="ng", align_bytes=64)
-            nc.vector.tensor_tensor(
-                out=ng[:],
-                in0=pr[:].rearrange("p c s e -> p (c s e)"),
-                in1=w_g[:].rearrange("p c j -> p (c j)"),
+        def add_cols(eng, b, lo, hi):
+            if ("ng", b) not in T:
+                T["ng", b] = work.tile([P, P, 16], BF16, name="ng", tag="ng", align_bytes=64)
+            eng.tensor_tensor(
+                out=T["ng", b][:, lo:hi, :].rearrange("p c j -> p (c j)"),
+                in0=T["pr", b][:, lo:hi, :, :].rearrange("p c s e -> p (c s e)"),
+                in1=w_g[:, lo:hi, :].rearrange("p c j -> p (c j)"),
                 op=ADD,
             )
-            state[("n", b)] = ng
 
-        def quant_w(b):
-            ng = state[("n", b)]
+        def A_pool(b):
+            if ok(b) and b > 0 and POOL_C > 0:
+                add_cols(nc.gpsimd, b, 0, POOL_C)
+
+        def A_dve(b):
+            if ok(b):
+                add_cols(nc.vector, b, POOL_C if b > 0 else 0, P)
+
+        def QN(b):
+            if not ok(b):
+                return
             ncod = work.tile([P, IN], U32, name="ncod", tag="ncod", align_bytes=64)
             nsc = work.tile([P, IN], U8, name="nsc", tag="nsc", align_bytes=64)
-            nc.vector.quantize_mx(out=ncod[:].bitcast(E4), scales=nsc[:], in_=ng[:])
-            state[("q", b)] = (ncod, nsc)
+            nc.vector.quantize_mx(
+                out=ncod[:].bitcast(E4), scales=nsc[:], in_=T["ng", b][:].rearrange("p c j -> p (c j)")
+            )
+            T["nq", b] = (ncod, nsc)
 
-        def stage_mm(b):
-            gg, gc, gs = state[("g", b)]
-            ncod, nsc = state[("q", b)]
-            out_v = out[b].rearrange("(p t) i -> p t i", t=TT)
-            for h in range(2):
-                o_sb = stage.tile([P, 4, IN], F32, name="o_sb", tag="o")
-                for r in range(4):
-                    t = 4 * h + r
-                    acc = ps_o.tile([P, IN], F32, name="acc", tag="acc")
-                    nc.tensor.matmul_mx(
-                        out=acc[:],
-                        lhsT=gc[:, t * P : (t + 1) * P].bitcast(E5),
-                        lhsT_scale=gs[:, t * P : (t + 1) * P],
-                        rhs=ncod[:].bitcast(E4),
-                        rhs_scale=nsc[:],
-                        start=True,
-                        stop=True,
-                    )
-                    nc.scalar.copy(out=o_sb[:, r, :], in_=acc[:])
-                nc.gpsimd.dma_start(out=out_v[:, 4 * h : 4 * h + 4, :], in_=o_sb[:])
+        def MX(b, t):
+            if not ok(b):
+                return
+            gc, gs = T["gq", b]
+            ncod, nsc = T["nq", b]
+            acc = ps_o.tile([P, IN], F32, name="acc", tag="acc")
+            nc.tensor.matmul_mx(
+                out=acc[:],
+                lhsT=gc[:, t * P : (t + 1) * P].bitcast(E5),
+                lhsT_scale=gs[:, t * P : (t + 1) * P],
+                rhs=ncod[:].bitcast(E4),
+                rhs_scale=nsc[:],
+                start=True,
+                stop=True,
+            )
+            T["acc", b, t] = acc
 
-        def stage_a(b):
-            stage_g(b)
-            stage_w(b)
-            quant_g(b)
-            add_w(b)
-            quant_w(b)
+        def O(b, t):
+            if t == 0:
+                T["o", b] = stage.tile([P, TT, IN], F32, name="o_sb", tag="o")
+            if t in vector_rows(b):
+                nc.vector.tensor_copy(out=T["o", b][:, t, :], in_=T["acc", b, t][:])
+            else:
+                nc.scalar.copy(out=T["o", b][:, t, :], in_=T["acc", b, t][:])
+            if t % 4 == 3:
+                lo = t - 3
+                nc.sync.dma_start(
+                    out=out[b].rearrange("(p t) i -> p t i", t=TT)[:, lo : t + 1, :],
+                    in_=T["o", b][:, lo : t + 1, :],
+                )
 
-        stage_g(0)
-        sig_g = prep_const(s_raw, "sig_g")
-        stage_w(0)
-        w_g = prep_const(w_raw, "w_g")
-        quant_g(0)
-        add_w(0)
-        quant_w(0)
-        for b in range(B):
-            if b + 1 < B:
-                stage_a(b + 1)
-            stage_mm(b)
+        load_w("s", sigma_weight)
+        load_w(0, weight_epsilon[0])
+        load_w("w", weight)
+        load_g(0, 0, 4)
+        load_g(0, 4, 8)
+        for b in range(1, EARLY):
+            load_w(b, weight_epsilon[b])
+            load_g(b, 0, 8)
+
+        te("s", 0, ps_o, "acc")
+        te("s", 1, ps_o, "acc")
+        PC("s", 0, sig_g)
+        PC("s", 1, sig_g)
+        TE(0, 0)
+        TE(0, 1)
+        M(0, 0)
+        M(0, 1)
+        te("w", 0, ps_o, "acc")
+        te("w", 1, ps_o, "acc")
+        PC("w", 0, w_g)
+        PC("w", 1, w_g)
+        TG(0, 0)
+        TG(0, 1)
+        TG(0, 2)
+        G(0, 0)
+        TG(0, 3)
+        G(0, 1)
+        G(0, 2)
+        G(0, 3)
+        A_dve(0)
+        QG(0)
+        QN(0)
+        for b in range(EARLY, B):
+            load_w(b, weight_epsilon[b])
+            load_g(b, 0, 8)
+        TE(1, 0)
+        TE(1, 1)
+        TG(1, 0)
+        TG(1, 1)
+        TG(1, 2)
+        MX(0, 0)
+        MX(0, 1)
+        MX(0, 2)
+        M(1, 0)
+        M(1, 1)
+        A_pool(1)
+        G(1, 0)
+        TG(1, 3)
+        TE(2, 0)
+        TE(2, 1)
+
+        for p in range(B):
+            G(p + 1, 1)
+            TG(p + 2, 0)
+            G(p + 1, 2)
+            TG(p + 2, 1)
+            G(p + 1, 3)
+            TG(p + 2, 2)
+            M(p + 2, 0)
+            M(p + 2, 1)
+            A_dve(p + 1)
+            QG(p + 1)
+            QN(p + 1)
+            A_pool(p + 2)
+            for t in range(5):
+                O(p, t)
+                MX(p, t + 3)
+            TE(p + 3, 0)
+            TE(p + 3, 1)
+            O(p, 5)
+            G(p + 2, 0)
+            TG(p + 2, 3)
+            MX(p + 1, 0)
+            O(p, 6)
+            MX(p + 1, 1)
+            O(p, 7)
+            MX(p + 1, 2)

@@ -18,14 +18,21 @@ TT = N // P
 WT = IN // P
 MULT = mybir.AluOpType.mult
 ADD = mybir.AluOpType.add
-POOL_C = 64
+POOL_C = 96
 EARLY = 6
 
 
 def vector_rows(b):
     if b == B - 1:
         return (1, 3, 5, 7)
-    return (7,)
+    return (6, 7)
+
+
+def store_from(b, t):
+    step = 8 if b <= 4 else 4
+    if t % step == step - 1:
+        return t - step + 1
+    return -1
 
 
 def tile_noisylinear_t_kernel(
@@ -183,8 +190,8 @@ def tile_noisylinear_t_kernel(
                 nc.vector.tensor_copy(out=T["o", b][:, t, :], in_=T["acc", b, t][:])
             else:
                 nc.scalar.copy(out=T["o", b][:, t, :], in_=T["acc", b, t][:])
-            if t % 4 == 3:
-                lo = t - 3
+            lo = store_from(b, t)
+            if lo >= 0:
                 nc.sync.dma_start(
                     out=out[b].rearrange("(p t) i -> p t i", t=TT)[:, lo : t + 1, :],
                     in_=T["o", b][:, lo : t + 1, :],

@@ -19,7 +19,9 @@ WT = IN // P
 MULT = mybir.AluOpType.mult
 ADD = mybir.AluOpType.add
 POOL_C = 96
-EARLY = 6
+GQ = 4
+SQ = 2
+PAIRED = 4
 
 
 def vector_rows(b):
@@ -28,11 +30,12 @@ def vector_rows(b):
     return (6, 7)
 
 
-def store_from(b, t):
-    step = 8 if b <= 4 else 4
-    if t % step == step - 1:
-        return t - step + 1
-    return -1
+def store_after(b, t):
+    if b < PAIRED:
+        return (b - 1, 2, 0, TT) if (b % 2 == 1 and t == TT - 1) else None
+    if b < B - 1:
+        return (b, 1, 0, TT) if t == TT - 1 else None
+    return (b, 1, t - 3, 4) if t % 4 == 3 else None
 
 
 def tile_noisylinear_t_kernel(
@@ -41,10 +44,12 @@ def tile_noisylinear_t_kernel(
     nc = tc.nc
     with ExitStack() as ctx:
         const = ctx.enter_context(tc.tile_pool(name="const", bufs=1))
-        gload = ctx.enter_context(tc.tile_pool(name="gload", bufs=7))
-        eload = ctx.enter_context(tc.tile_pool(name="eload", bufs=8))
+        big = ctx.enter_context(tc.tile_pool(name="big", bufs=4))
+        eload1 = ctx.enter_context(tc.tile_pool(name="eload1", bufs=3))
+        eload2 = ctx.enter_context(tc.tile_pool(name="eload2", bufs=2))
+        eload3 = ctx.enter_context(tc.tile_pool(name="eload3", bufs=1))
+        eload = {1: eload1, 2: eload2, 3: eload3}
         work = ctx.enter_context(tc.tile_pool(name="work", bufs=2))
-        stage = ctx.enter_context(tc.tile_pool(name="stage", bufs=4))
         ps_g = ctx.enter_context(tc.psum_pool(name="ps_g", bufs=3))
         ps_e = ctx.enter_context(tc.psum_pool(name="ps_e", bufs=2))
         ps_o = ctx.enter_context(tc.psum_pool(name="ps_o", bufs=3))
@@ -60,25 +65,48 @@ def tile_noisylinear_t_kernel(
         def ok(b):
             return 0 <= b < B
 
-        def load_g(b, lo, hi):
-            if lo == 0:
-                T["g", b] = gload.tile([P, TT, OUT], BF16, name="g_t", tag="g")
+        def load_g_part(b, t0, t1):
+            q = b // GQ
+            if ("gt", q) not in T:
+                T["gt", q] = big.tile([P, GQ * TT, OUT], BF16, name="g_t", tag="big")
+            lo = (b - q * GQ) * TT
             nc.sync.dma_start(
-                out=T["g", b][:, lo:hi, :],
-                in_=grad_out[b].rearrange("(p t) k -> p t k", t=TT)[:, lo:hi, :],
+                out=T["gt", q][:, lo + t0 : lo + t1, :],
+                in_=grad_out[b].rearrange("(p t) k -> p t k", t=TT)[:, t0:t1, :],
+            )
+
+        def load_g(b0, b1):
+            q = b0 // GQ
+            if ("gt", q) not in T:
+                T["gt", q] = big.tile([P, GQ * TT, OUT], BF16, name="g_t", tag="big")
+            lo, hi = (b0 - q * GQ) * TT, (b1 - q * GQ) * TT
+            nc.sync.dma_start(
+                out=T["gt", q][:, lo:hi, :].rearrange("p (b t) k -> p b (t k)", t=TT),
+                in_=grad_out[b0:b1].rearrange("b (p t) k -> p b (t k)", t=TT),
             )
 
         def load_w(key, src):
-            T["e", key] = eload.tile([P, WT, OUT], BF16, name="e_t", tag="e")
-            nc.sync.dma_start(out=T["e", key][:], in_=src.rearrange("(p t) k -> p t k", t=WT))
+            e_t = eload[1].tile([P, WT, OUT], BF16, name="e_t", tag="e")
+            T["e", key] = (e_t, 0)
+            nc.sync.dma_start(out=e_t[:], in_=src.rearrange("(p t) k -> p t k", t=WT))
+
+        def load_e(b0, b1):
+            e_t = eload[b1 - b0].tile([P, (b1 - b0) * WT, OUT], BF16, name="e_t", tag="e")
+            for b in range(b0, b1):
+                T["e", b] = (e_t, (b - b0) * WT)
+            nc.sync.dma_start(
+                out=e_t[:].rearrange("p (b t) k -> p b (t k)", t=WT),
+                in_=weight_epsilon[b0:b1].rearrange("b (p t) k -> p b (t k)", t=WT),
+            )
 
         def te(key, h, pool, tag):
-            src32 = T["e", key][:].bitcast(F32)
+            e_t, t0 = T["e", key]
+            src32 = e_t[:].bitcast(F32)
             xe = pool.tile([P, 512], F32, name="xe", tag=tag)
             for s in range(4):
                 t, u = (4 * h + s) // 2, s % 2
                 nc.tensor.transpose(
-                    xe[:, s * P : (s + 1) * P], src32[:, t, u * P : (u + 1) * P], ident[:]
+                    xe[:, s * P : (s + 1) * P], src32[:, t0 + t, u * P : (u + 1) * P], ident[:]
                 )
             T["xe", key, h] = xe
 
@@ -95,10 +123,10 @@ def tile_noisylinear_t_kernel(
         def TG(b, j):
             if not ok(b):
                 return
-            g32 = T["g", b][:].bitcast(F32)
+            g32 = T["gt", b // GQ][:].bitcast(F32)
             xg = ps_g.tile([P, 512], F32, name="xg", tag="xg")
             for s in range(4):
-                t, u = 2 * j + s // 2, s % 2
+                t, u = (b % GQ) * TT + 2 * j + s // 2, s % 2
                 nc.tensor.transpose(
                     xg[:, s * P : (s + 1) * P], g32[:, t, u * P : (u + 1) * P], ident[:]
                 )
@@ -184,27 +212,43 @@ def tile_noisylinear_t_kernel(
             T["acc", b, t] = acc
 
         def O(b, t):
-            if t == 0:
-                T["o", b] = stage.tile([P, TT, IN], F32, name="o_sb", tag="o")
+            if t == 0 and b % SQ == 0:
+                T["o", b // SQ] = big.tile([P, SQ * TT, IN], F32, name="o_sb", tag="big")
+            o_sb = T["o", b // SQ]
+            r = (b % SQ) * TT + t
             if t in vector_rows(b):
-                nc.vector.tensor_copy(out=T["o", b][:, t, :], in_=T["acc", b, t][:])
+                nc.vector.tensor_copy(out=o_sb[:, r, :], in_=T["acc", b, t][:])
             else:
-                nc.scalar.copy(out=T["o", b][:, t, :], in_=T["acc", b, t][:])
-            lo = store_from(b, t)
-            if lo >= 0:
-                nc.sync.dma_start(
-                    out=out[b].rearrange("(p t) i -> p t i", t=TT)[:, lo : t + 1, :],
-                    in_=T["o", b][:, lo : t + 1, :],
-                )
+                nc.scalar.copy(out=o_sb[:, r, :], in_=T["acc", b, t][:])
+            st = store_after(b, t)
+            if st is not None:
+                b0, nb, t0, nt = st
+                r0 = (b0 % SQ) * TT + t0
+                if nt == TT:
+                    nc.sync.dma_start(
+                        out=out[b0 : b0 + nb].rearrange("b (p t) i -> p b (t i)", t=TT),
+                        in_=o_sb[:, r0 : r0 + nb * TT, :].rearrange("p (b t) i -> p b (t i)", t=TT),
+                    )
+                else:
+                    nc.sync.dma_start(
+                        out=out[b0].rearrange("(p t) i -> p t i", t=TT)[:, t0 : t0 + nt, :],
+                        in_=o_sb[:, r0 : r0 + nt, :],
+                    )
 
         load_w("s", sigma_weight)
-        load_w(0, weight_epsilon[0])
+        load_e(0, 1)
         load_w("w", weight)
-        load_g(0, 0, 4)
-        load_g(0, 4, 8)
-        for b in range(1, EARLY):
-            load_w(b, weight_epsilon[b])
-            load_g(b, 0, 8)
+        load_g_part(0, 0, 4)
+        load_g_part(0, 4, 8)
+        load_e(1, 3)
+        load_g(1, 2)
+        load_g(2, 3)
+        load_e(3, 5)
+        load_g(3, 4)
+        load_g(4, 5)
+        load_e(5, 8)
+        load_g(5, 6)
+        load_g(6, 8)
 
         te("s", 0, ps_o, "acc")
         te("s", 1, ps_o, "acc")
@@ -229,9 +273,6 @@ def tile_noisylinear_t_kernel(
         A_dve(0)
         QG(0)
         QN(0)
-        for b in range(EARLY, B):
-            load_w(b, weight_epsilon[b])
-            load_g(b, 0, 8)
         TE(1, 0)
         TE(1, 1)
         TG(1, 0)

@@ -21,7 +21,7 @@ ADD = mybir.AluOpType.add
 POOL_C = 96
 GQ = 4
 SQ = 2
-PAIRED = 4
+PAIRED = 2
 
 
 def vector_rows(b):
@@ -64,16 +64,6 @@ def tile_noisylinear_t_kernel(
 
         def ok(b):
             return 0 <= b < B
-
-        def load_g_part(b, t0, t1):
-            q = b // GQ
-            if ("gt", q) not in T:
-                T["gt", q] = big.tile([P, GQ * TT, OUT], BF16, name="g_t", tag="big")
-            lo = (b - q * GQ) * TT
-            nc.sync.dma_start(
-                out=T["gt", q][:, lo + t0 : lo + t1, :],
-                in_=grad_out[b].rearrange("(p t) k -> p t k", t=TT)[:, t0:t1, :],
-            )
 
         def load_g(b0, b1):
             q = b0 // GQ
@@ -238,16 +228,14 @@ def tile_noisylinear_t_kernel(
         load_w("s", sigma_weight)
         load_e(0, 1)
         load_w("w", weight)
-        load_g_part(0, 0, 4)
-        load_g_part(0, 4, 8)
+        load_g(0, 1)
         load_e(1, 3)
         load_g(1, 2)
         load_g(2, 3)
         load_e(3, 5)
         load_g(3, 4)
-        load_g(4, 5)
+        load_g(4, 6)
         load_e(5, 8)
-        load_g(5, 6)
         load_g(6, 8)
 
         te("s", 0, ps_o, "acc")

from contextlib import ExitStack

import concourse.mybir as mybir
from concourse.masks import make_identity

B, N, IN, OUT = 8, 1024, 512, 512
FLOPS = 2 * B * N * IN * OUT
BYTES = B * N * OUT * 2 + B * IN * OUT * 2 + 2 * IN * OUT * 2 + B * N * IN * 4

F32 = mybir.dt.float32
BF16 = mybir.dt.bfloat16
U32 = mybir.dt.uint32
U8 = mybir.dt.uint8
E4 = mybir.dt.float8_e4m3fn_x4
E5 = mybir.dt.float8_e5m2_x4
P = 128
TT = N // P
WT = IN // P
MULT = mybir.AluOpType.mult
ADD = mybir.AluOpType.add
POOL_C = 96
GQ = 4
SQ = 2
PAIRED = 2


def vector_rows(b):
    if b == B - 1:
        return (1, 3, 5, 7)
    return (6, 7)


def store_after(b, t):
    if b < PAIRED:
        return (b - 1, 2, 0, TT) if (b % 2 == 1 and t == TT - 1) else None
    if b < B - 1:
        return (b, 1, 0, TT) if t == TT - 1 else None
    return (b, 1, t - 3, 4) if t % 4 == 3 else None


def tile_noisylinear_t_kernel(
    tc, x, weight, bias, sigma_weight, sigma_bias, weight_epsilon, bias_epsilon, grad_out, out
):
    nc = tc.nc
    with ExitStack() as ctx:
        const = ctx.enter_context(tc.tile_pool(name="const", bufs=1))
        big = ctx.enter_context(tc.tile_pool(name="big", bufs=4))
        eload1 = ctx.enter_context(tc.tile_pool(name="eload1", bufs=3))
        eload2 = ctx.enter_context(tc.tile_pool(name="eload2", bufs=2))
        eload3 = ctx.enter_context(tc.tile_pool(name="eload3", bufs=1))
        eload = {1: eload1, 2: eload2, 3: eload3}
        work = ctx.enter_context(tc.tile_pool(name="work", bufs=2))
        ps_g = ctx.enter_context(tc.psum_pool(name="ps_g", bufs=3))
        ps_e = ctx.enter_context(tc.psum_pool(name="ps_e", bufs=2))
        ps_o = ctx.enter_context(tc.psum_pool(name="ps_o", bufs=3))
        ctx.enter_context(tc.manual_schedule())

        ident = const.tile([P, P], F32, name="ident")
        make_identity(nc, ident[:])
        sig_g = const.tile([P, P, 16], BF16, name="sig_g", align_bytes=64)
        w_g = const.tile([P, P, 16], BF16, name="w_g", align_bytes=64)

        T = {}

        def ok(b):
            return 0 <= b < B

        def load_g(b0, b1):
            q = b0 // GQ
            if ("gt", q) not in T:
                T["gt", q] = big.tile([P, GQ * TT, OUT], BF16, name="g_t", tag="big")
            lo, hi = (b0 - q * GQ) * TT, (b1 - q * GQ) * TT
            nc.sync.dma_start(
                out=T["gt", q][:, lo:hi, :].rearrange("p (b t) k -> p b (t k)", t=TT),
                in_=grad_out[b0:b1].rearrange("b (p t) k -> p b (t k)", t=TT),
            )

        def load_w(key, src):
            e_t = eload[1].tile([P, WT, OUT], BF16, name="e_t", tag="e")
            T["e", key] = (e_t, 0)
            nc.sync.dma_start(out=e_t[:], in_=src.rearrange("(p t) k -> p t k", t=WT))

        def load_e(b0, b1):
            e_t = eload[b1 - b0].tile([P, (b1 - b0) * WT, OUT], BF16, name="e_t", tag="e")
            for b in range(b0, b1):
                T["e", b] = (e_t, (b - b0) * WT)
            nc.sync.dma_start(
                out=e_t[:].rearrange("p (b t) k -> p b (t k)", t=WT),
                in_=weight_epsilon[b0:b1].rearrange("b (p t) k -> p b (t k)", t=WT),
            )

        def te(key, h, pool, tag):
            e_t, t0 = T["e", key]
            src32 = e_t[:].bitcast(F32)
            xe = pool.tile([P, 512], F32, name="xe", tag=tag)
            for s in range(4):
                t, u = (4 * h + s) // 2, s % 2
                nc.tensor.transpose(
                    xe[:, s * P : (s + 1) * P], src32[:, t0 + t, u * P : (u + 1) * P], ident[:]
                )
            T["xe", key, h] = xe

        def TE(b, h):
            if ok(b):
                te(b, h, ps_e, "xe")

        def PC(key, h, dst):
            nc.scalar.copy(
                out=dst[:].bitcast(F32)[:, :, 4 * h : 4 * h + 4],
                in_=T["xe", key, h][:].rearrange("p (s c) -> p c s", s=4),
            )

        def TG(b, j):
            if not ok(b):
                return
            g32 = T["gt", b // GQ][:].bitcast(F32)
            xg = ps_g.tile([P, 512], F32, name="xg", tag="xg")
            for s in range(4):
                t, u = (b % GQ) * TT + 2 * j + s // 2, s % 2
                nc.tensor.transpose(
                    xg[:, s * P : (s + 1) * P], g32[:, t, u * P : (u + 1) * P], ident[:]
                )
            T["xg", b, j] = xg

        def G(b, j):
            if not ok(b):
                return
            if j == 0:
                T["gg", b] = work.tile([P, TT, P, 4], BF16, name="gg", tag="gg", align_bytes=64)
            nc.scalar.copy(
                out=T["gg", b][:].bitcast(F32)[:, 2 * j : 2 * j + 2, :, :],
                in_=T["xg", b, j][:].rearrange("p (t u c) -> p t c u", t=2, u=2),
            )

        def QG(b):
            if not ok(b):
                return
            gc = work.tile([P, N], U32, name="gc", tag="gc", align_bytes=64)
            gs = work.tile([P, N], U8, name="gs", tag="gs", align_bytes=64)
            nc.vector.quantize_mx(
                out=gc[:].bitcast(E5),
                scales=gs[:],
                in_=T["gg", b][:].rearrange("p t c j -> p (t c j)"),
            )
            T["gq", b] = (gc, gs)

        def M(b, h):
            if not ok(b):
                return
            if h == 0:
                T["pr", b] = work.tile([P, P, 8, 2], F32, name="pr", tag="pr")
            nc.vector.tensor_tensor(
                out=T["pr", b][:, :, 4 * h : 4 * h + 4, :],
                in0=T["xe", b, h][:].bitcast(BF16).rearrange("p (s c e) -> p c s e", s=4, e=2),
                in1=sig_g[:, :, 8 * h : 8 * h + 8].rearrange("p c (s e) -> p c s e", e=2),
                op=MULT,
            )

        def add_cols(eng, b, lo, hi):
            if ("ng", b) not in T:
                T["ng", b] = work.tile([P, P, 16], BF16, name="ng", tag="ng", align_bytes=64)
            eng.tensor_tensor(
                out=T["ng", b][:, lo:hi, :].rearrange("p c j -> p (c j)"),
                in0=T["pr", b][:, lo:hi, :, :].rearrange("p c s e -> p (c s e)"),
                in1=w_g[:, lo:hi, :].rearrange("p c j -> p (c j)"),
                op=ADD,
            )

        def A_pool(b):
            if ok(b) and b > 0 and POOL_C > 0:
                add_cols(nc.gpsimd, b, 0, POOL_C)

        def A_dve(b):
            if ok(b):
                add_cols(nc.vector, b, POOL_C if b > 0 else 0, P)

        def QN(b):
            if not ok(b):
                return
            ncod = work.tile([P, IN], U32, name="ncod", tag="ncod", align_bytes=64)
            nsc = work.tile([P, IN], U8, name="nsc", tag="nsc", align_bytes=64)
            nc.vector.quantize_mx(
                out=ncod[:].bitcast(E4), scales=nsc[:], in_=T["ng", b][:].rearrange("p c j -> p (c j)")
            )
            T["nq", b] = (ncod, nsc)

        def MX(b, t):
            if not ok(b):
                return
            gc, gs = T["gq", b]
            ncod, nsc = T["nq", b]
            acc = ps_o.tile([P, IN], F32, name="acc", tag="acc")
            nc.tensor.matmul_mx(
                out=acc[:],
                lhsT=gc[:, t * P : (t + 1) * P].bitcast(E5),
                lhsT_scale=gs[:, t * P : (t + 1) * P],
                rhs=ncod[:].bitcast(E4),
                rhs_scale=nsc[:],
                start=True,
                stop=True,
            )
            T["acc", b, t] = acc

        def O(b, t):
            if t == 0 and b % SQ == 0:
                T["o", b // SQ] = big.tile([P, SQ * TT, IN], F32, name="o_sb", tag="big")
            o_sb = T["o", b // SQ]
            r = (b % SQ) * TT + t
            if t in vector_rows(b):
                nc.vector.tensor_copy(out=o_sb[:, r, :], in_=T["acc", b, t][:])
            else:
                nc.scalar.copy(out=o_sb[:, r, :], in_=T["acc", b, t][:])
            st = store_after(b, t)
            if st is not None:
                b0, nb, t0, nt = st
                r0 = (b0 % SQ) * TT + t0
                if nt == TT:
                    nc.sync.dma_start(
                        out=out[b0 : b0 + nb].rearrange("b (p t) i -> p b (t i)", t=TT),
                        in_=o_sb[:, r0 : r0 + nb * TT, :].rearrange("p (b t) i -> p b (t i)", t=TT),
                    )
                else:
                    nc.sync.dma_start(
                        out=out[b0].rearrange("(p t) i -> p t i", t=TT)[:, t0 : t0 + nt, :],
                        in_=o_sb[:, r0 : r0 + nt, :],
                    )

        load_w("s", sigma_weight)
        load_e(0, 1)
        load_w("w", weight)
        load_g(0, 1)
        load_e(1, 3)
        load_g(1, 2)
        load_g(2, 3)
        load_e(3, 5)
        load_g(3, 4)
        load_g(4, 6)
        load_e(5, 8)
        load_g(6, 8)

        te("s", 0, ps_o, "acc")
        te("s", 1, ps_o, "acc")
        PC("s", 0, sig_g)
        PC("s", 1, sig_g)
        TE(0, 0)
        TE(0, 1)
        M(0, 0)
        M(0, 1)
        te("w", 0, ps_o, "acc")
        te("w", 1, ps_o, "acc")
        PC("w", 0, w_g)
        PC("w", 1, w_g)
        TG(0, 0)
        TG(0, 1)
        TG(0, 2)
        G(0, 0)
        TG(0, 3)
        G(0, 1)
        G(0, 2)
        G(0, 3)
        A_dve(0)
        QG(0)
        QN(0)
        TE(1, 0)
        TE(1, 1)
        TG(1, 0)
        TG(1, 1)
        TG(1, 2)
        MX(0, 0)
        MX(0, 1)
        MX(0, 2)
        M(1, 0)
        M(1, 1)
        A_pool(1)
        G(1, 0)
        TG(1, 3)
        TE(2, 0)
        TE(2, 1)

        for p in range(B):
            G(p + 1, 1)
            TG(p + 2, 0)
            G(p + 1, 2)
            TG(p + 2, 1)
            G(p + 1, 3)
            TG(p + 2, 2)
            M(p + 2, 0)
            M(p + 2, 1)
            A_dve(p + 1)
            QG(p + 1)
            QN(p + 1)
            A_pool(p + 2)
            for t in range(5):
                O(p, t)
                MX(p, t + 3)
            TE(p + 3, 0)
            TE(p + 3, 1)
            O(p, 5)
            G(p + 2, 0)
            TG(p + 2, 3)
            MX(p + 1, 0)
            O(p, 6)
            MX(p + 1, 1)
            O(p, 7)
            MX(p + 1, 2)
